import numpy as np
import ml_dtypes


def mxq(x, axis, fmt="e4m3"):
    dtype, down = {"e4m3": (ml_dtypes.float8_e4m3fn, 7), "e5m2": (ml_dtypes.float8_e5m2, 14)}[fmt]
    v = np.moveaxis(np.asarray(x, np.float32).astype(ml_dtypes.bfloat16).astype(np.float64), axis, -1)
    blocks = v.reshape(v.shape[:-1] + (-1, 32))
    amax = np.abs(blocks).max(-1, keepdims=True)
    byte = np.maximum(np.where(amax > 0, np.frexp(amax)[1] - 1 + 127, 0) - down, 1)
    scale = np.exp2(byte - 127.0)
    codes = (blocks / scale).astype(np.float32).astype(dtype).astype(np.float64)
    return np.moveaxis((codes * scale).reshape(v.shape), -1, axis)


WIDE = False


def mx_kscale(k):
    if not WIDE:
        return np.ones(k)
    levels = np.array([20, -20, 10, -10, 0])
    a = np.random.permutation(np.resize(levels, k // 512 * 4)).reshape(k // 512, 4)
    idx = np.arange(k)
    return np.exp2(a[idx // 512, idx % 128 // 32])


BF16 = ml_dtypes.bfloat16


def bf(x):
    return np.asarray(x, np.float32).astype(BF16)


def f64(x):
    return np.asarray(x).astype(np.float64)


B, H0, C0, C1, C2, NA, NO = 4, 32, 512, 512, 1024, 4, 128
H1, H2 = H0 // 2, H0 // 4
O = NA * NO
T = B * H0 * H0
R0 = NA * H0 * H0
R = NA * (H0 * H0 + H1 * H1 + H2 * H2)


def sigmoid(v):
    return 1.0 / (1.0 + np.exp(-v))


def _draw_level(c, h):
    f = bf(np.random.standard_normal((B, c, h, h)))
    w = bf(np.random.standard_normal((O, c)) / np.sqrt(c))
    b = bf(np.random.standard_normal(O) * 0.5)
    return f, w, b


def setup_inputs():
    s = mx_kscale(T).reshape(B, H0, H0)
    f00, w0, b0 = _draw_level(C0, H0)
    f1, w1, b1 = _draw_level(C1, H1)
    f2, w2, b2 = _draw_level(C2, H2)
    anchors = bf(1.0 + 4.0 * np.random.random((3, NA, 2)))
    g = np.random.standard_normal((B, R, NO)) * np.exp2(np.random.randint(-12, 1, (B, R, 1)))
    g[:, :R0] = (g[:, :R0].reshape(B, NA, H0, H0, NO) / s[:, None, :, :, None]).reshape(B, R0, NO)
    y0 = (f64(w0) @ f64(f00).reshape(B, C0, H0 * H0) + f64(b0)[None, :, None]).reshape(B, O, H0, H0)
    f0 = bf(f64(f00) * s[:, None, :, :])
    return {"f0": f0, "f1": f1, "f2": f2, "w0": w0, "b0": b0, "w1": w1, "b1": b1, "w2": w2, "b2": b2,
            "anchors": anchors, "y0": np.asarray(y0, np.float32), "grad_out": bf(g)}


def reference(f0, f1, f2, w0, b0, w1, b1, w2, b2, anchors, y0, grad_out):
    g = f64(grad_out)[:, :R0].reshape(B, NA, H0 * H0, NO)
    sg = sigmoid(f64(y0).reshape(B, NA, NO, H0 * H0)[:, :, 0:4].transpose(0, 1, 3, 2))
    a0 = f64(anchors)[0]
    sxy, swh = sg[..., 0:2], sg[..., 2:4]
    dxy = g[..., 0:2] * (2.0 * sxy * (1.0 - sxy))
    dwh = g[..., 2:4] * (8.0 * swh * swh * (1.0 - swh)) * a0[None, :, None, :]
    dy = np.concatenate([dxy, dwh, g[..., 4:]], axis=-1)
    dy = dy.transpose(0, 2, 1, 3).reshape(T, O)
    f = f64(f0).reshape(B, C0, H0 * H0).transpose(0, 2, 1).reshape(T, C0)
    return mxq(dy, 0, "e5m2").T @ mxq(f, 0, "e4m3")

@@ -1,0 +1,171 @@
+from contextlib import ExitStack
+
+import concourse.masks as masks
+import concourse.mybir as mybir
+
+F32 = mybir.dt.float32
+BF16 = mybir.dt.bfloat16
+U32 = mybir.dt.uint32
+U8 = mybir.dt.uint8
+E4M3_X4 = mybir.dt.float8_e4m3fn_x4
+E5M2_X4 = mybir.dt.float8_e5m2_x4
+ALU = mybir.AluOpType
+ACT = mybir.ActivationFunctionType
+
+P = 128
+PACK = 4
+K_PASS = P * PACK
+B = 4
+C = 512
+MAP = 32 * 32
+HALVES = MAP // K_PASS
+NA = 4
+NO = 128
+NS = 4
+C_PER_PART = C // P
+WORDS = K_PASS // 2
+ROWS_PER_LOAD = B * NA
+
+FLOPS = 2 * B * MAP * NA * NO * C
+BYTES = 2 * B * C * MAP + 2 * B * NA * MAP * NO + 4 * B * NA * NS * MAP + 2 * NA * 2 + 4 * NA * NO * C
+
+
+def tile_head_v_kernel(tc, f0, f1, f2, w0, b0, w1, b1, w2, b2, anchors, y0, grad_out, out):
+    nc = tc.nc
+    with ExitStack() as ctx:
+        const = ctx.enter_context(tc.tile_pool(name="const", bufs=1))
+        f_load = ctx.enter_context(tc.tile_pool(name="f_load", bufs=B))
+        f_pass = ctx.enter_context(tc.tile_pool(name="f_pass", bufs=B * HALVES))
+        g_piece = ctx.enter_context(tc.tile_pool(name="g_piece", bufs=B * NA))
+        result = ctx.enter_context(tc.tile_pool(name="result", bufs=NA))
+        acc_banks = ctx.enter_context(tc.psum_pool(name="acc_banks", bufs=1))
+        flip_banks = ctx.enter_context(tc.psum_pool(name="flip_banks", bufs=4))
+
+        ident = const.tile([P, P], F32)
+        masks.make_identity(nc, ident[:])
+
+        y_rows = y0.rearrange("n (a j) u v -> (n a) j (u v)", j=NO)
+        y_sb = const.tile([P, K_PASS], F32)
+        for j in range(NS):
+            for h in range(HALVES):
+                first = (j * HALVES + h) * ROWS_PER_LOAD
+                queue = nc.scalar if h == 0 else nc.gpsimd
+                queue.dma_start(
+                    out=y_sb[first : first + ROWS_PER_LOAD, :],
+                    in_=y_rows[:, j, h * K_PASS : (h + 1) * K_PASS],
+                )
+        anc = const.tile([P, NA * 2], BF16)
+        nc.scalar.dma_start(out=anc[:], in_=anchors[0].rearrange("a w -> (a w)").partition_broadcast(P))
+
+        def load_f(n):
+            f_raw = f_load.tile([P, C_PER_PART * MAP], BF16)
+            nc.sync.dma_start(out=f_raw[:], in_=f0[n].rearrange("(p i) u v -> p (i u v)", i=C_PER_PART))
+            return f_raw
+
+        def load_g(n, a):
+            g_raw = g_piece.tile([P, HALVES, PACK, NO], BF16)
+            nc.sync.dma_start(
+                out=g_raw[:].rearrange("p h r j -> p h (r j)"),
+                in_=grad_out[n, a * MAP : (a + 1) * MAP, :].rearrange("(h p r) j -> p h (r j)", h=HALVES, r=PACK),
+            )
+            return g_raw
+
+        f_raws = [load_f(0)]
+        g_raws = []
+        for n in range(B):
+            if n + 1 < B:
+                f_raws.append(load_f(n + 1))
+            g_raws.append([load_g(n, a) for a in range(NA)])
+
+        sig = const.tile([P, PACK, P], F32)
+        nc.scalar.activation(out=sig[:], in_=y_sb[:].rearrange("q (p r) -> q r p", r=PACK), func=ACT.Sigmoid)
+        slope = const.tile([P, PACK, P], F32)
+        nc.vector.scalar_tensor_tensor(
+            out=slope[:], in0=sig[:], scalar=1.0, in1=sig[:], op0=ALU.subtract, op1=ALU.mult
+        )
+        nc.vector.scalar_tensor_tensor(
+            out=slope[P // 2 : P], in0=slope[P // 2 : P], scalar=-8.0, in1=sig[P // 2 : P], op0=ALU.mult, op1=ALU.mult
+        )
+        slope_t = flip_banks.tile([P, PACK, P], F32, tag="flip")
+        for r in range(PACK):
+            nc.tensor.transpose(out=slope_t[:, r, :], in_=slope[:, r, :], identity=ident[:])
+        factor = const.tile([P, PACK, NS, HALVES, B, NA], F32)
+        plain = P // 2
+        nc.vector.tensor_scalar(
+            out=factor[:].rearrange("p r j h n a -> p r (j h n a)")[:, :, 0:plain],
+            in0=slope_t[:, :, 0:plain],
+            scalar1=-2.0,
+            scalar2=None,
+            op0=ALU.mult,
+        )
+        per_field = HALVES * B * NA
+        for w in range(2):
+            nc.vector.tensor_tensor(
+                out=factor[:, :, 2 + w].rearrange("p r h n a -> p r (h n) a"),
+                in0=slope_t[:, :, plain + w * per_field : plain + (w + 1) * per_field].rearrange(
+                    "p r (x a) -> p r x a", a=NA
+                ),
+                in1=anc[:]
+                .rearrange("p (a w) -> p w a", w=2)[:, w, :]
+                .unsqueeze(1)
+                .unsqueeze(1)
+                .to_broadcast([P, PACK, HALVES * B, NA]),
+                op=ALU.mult,
+            )
+
+        def quantise_f(n, h):
+            words = f_raws[n][:].bitcast(F32).rearrange(
+                "c (i h p s) -> c i h s p", i=C_PER_PART, h=HALVES, p=P, s=2
+            )
+            f_grouped = f_pass.tile([P, C * PACK], BF16, align_bytes=64)
+            grouped_words = f_grouped[:].bitcast(F32).rearrange("p (c b x) -> p b c x", b=2, x=4)
+            for b in range(2):
+                flip = flip_banks.tile([P, 4, P], F32, tag="flip")
+                for x in range(4):
+                    nc.tensor.transpose(out=flip[:, x, :], in_=words[:, 2 * b + x // 2, h, x % 2, :], identity=ident[:])
+                nc.scalar.copy(out=grouped_words[:, b], in_=flip[:].rearrange("p x c -> p c x"))
+            f_codes = f_pass.tile([P, C], U32, align_bytes=64)
+            f_scales = f_pass.tile([P, C], U8, align_bytes=64)
+            nc.vector.quantize_mx(out=f_codes[:].bitcast(E4M3_X4), scales=f_scales[:], in_=f_grouped[:])
+            return f_codes, f_scales
+
+        def quantise_dy(n, a):
+            dy = g_piece.tile([P, HALVES, NO, PACK], BF16, align_bytes=64)
+            copier = nc.scalar.copy if a == 0 else nc.vector.tensor_copy
+            copier(out=dy[:], in_=g_raws[n][a][:].rearrange("p h r j -> p h j r"))
+            nc.vector.tensor_tensor(
+                out=dy[:, :, 0:NS, :],
+                in0=dy[:, :, 0:NS, :],
+                in1=factor[:, :, :, :, n, a].rearrange("p r j h -> p h j r"),
+                op=ALU.mult,
+            )
+            dy_codes = g_piece.tile([P, HALVES * NO], U32, align_bytes=64)
+            dy_scales = g_piece.tile([P, HALVES * NO], U8, align_bytes=64)
+            nc.vector.quantize_mx(
+                out=dy_codes[:].bitcast(E5M2_X4), scales=dy_scales[:], in_=dy[:].rearrange("p h j r -> p (h j r)")
+            )
+            return dy_codes, dy_scales
+
+        acc = [acc_banks.tile([P, C], F32, name="acc%d" % a) for a in range(NA)]
+        f_mx = [[quantise_f(0, h) for h in range(HALVES)]]
+        for n in range(B):
+            if n + 1 < B:
+                f_mx.append([quantise_f(n + 1, h) for h in range(HALVES)])
+            for a in range(NA):
+                dy_codes, dy_scales = quantise_dy(n, a)
+                for h in range(HALVES):
+                    f_codes, f_scales = f_mx[n][h]
+                    fields = slice(h * NO, (h + 1) * NO)
+                    nc.tensor.matmul_mx(
+                        out=acc[a][:],
+                        lhsT=dy_codes[:, fields].bitcast(E5M2_X4),
+                        lhsT_scale=dy_scales[:, fields],
+                        rhs=f_codes[:].bitcast(E4M3_X4),
+                        rhs_scale=f_scales[:],
+                        start=(n == 0 and h == 0),
+                        stop=(n == B - 1 and h == HALVES - 1),
+                    )
+                if n == B - 1:
+                    rows = result.tile([P, C], F32)
+                    nc.scalar.copy(out=rows[:], in_=acc[a][:])
+                    nc.sync.dma_start(out=out[a * NO : (a + 1) * NO, :], in_=rows[:])

@@ -22,9 +22,6 @@ HALVES = MAP // K_PASS
 NA = 4
 NO = 128
 NS = 4
-C_PER_PART = C // P
-WORDS = K_PASS // 2
-ROWS_PER_LOAD = B * NA
 
 FLOPS = 2 * B * MAP * NA * NO * C
 BYTES = 2 * B * C * MAP + 2 * B * NA * MAP * NO + 4 * B * NA * NS * MAP + 2 * NA * 2 + 4 * NA * NO * C
@@ -34,8 +31,8 @@ def tile_head_v_kernel(tc, f0, f1, f2, w0, b0, w1, b1, w2, b2, anchors, y0, grad
     nc = tc.nc
     with ExitStack() as ctx:
         const = ctx.enter_context(tc.tile_pool(name="const", bufs=1))
-        f_load = ctx.enter_context(tc.tile_pool(name="f_load", bufs=B))
-        f_pass = ctx.enter_context(tc.tile_pool(name="f_pass", bufs=B * HALVES))
+        f_load = ctx.enter_context(tc.tile_pool(name="f_load", bufs=B * 2))
+        f_image = ctx.enter_context(tc.tile_pool(name="f_image", bufs=B))
         g_piece = ctx.enter_context(tc.tile_pool(name="g_piece", bufs=B * NA))
         result = ctx.enter_context(tc.tile_pool(name="result", bufs=NA))
         acc_banks = ctx.enter_context(tc.psum_pool(name="acc_banks", bufs=1))
@@ -44,22 +41,19 @@ def tile_head_v_kernel(tc, f0, f1, f2, w0, b0, w1, b1, w2, b2, anchors, y0, grad
         ident = const.tile([P, P], F32)
         masks.make_identity(nc, ident[:])
 
-        y_rows = y0.rearrange("n (a j) u v -> (n a) j (u v)", j=NO)
+        y_rows = y0.rearrange("n (a j) u v -> (n a) j (u v)", j=NO)[:, 0:NS, :]
         y_sb = const.tile([P, K_PASS], F32)
-        for j in range(NS):
-            for h in range(HALVES):
-                first = (j * HALVES + h) * ROWS_PER_LOAD
-                queue = nc.scalar if h == 0 else nc.gpsimd
-                queue.dma_start(
-                    out=y_sb[first : first + ROWS_PER_LOAD, :],
-                    in_=y_rows[:, j, h * K_PASS : (h + 1) * K_PASS],
-                )
+        nc.sync.dma_start(out=y_sb[:], in_=y_rows.rearrange("q j (h k) -> q (j h) k", h=HALVES))
         anc = const.tile([P, NA * 2], BF16)
         nc.scalar.dma_start(out=anc[:], in_=anchors[0].rearrange("a w -> (a w)").partition_broadcast(P))
 
         def load_f(n):
-            f_raw = f_load.tile([P, C_PER_PART * MAP], BF16)
-            nc.sync.dma_start(out=f_raw[:], in_=f0[n].rearrange("(p i) u v -> p (i u v)", i=C_PER_PART))
+            channels = f0[n].rearrange("(p b i) u v -> p b (i u v)", b=2, i=2)
+            f_raw = []
+            for b in range(2):
+                f_half = f_load.tile([P, 2 * MAP], BF16)
+                nc.sync.dma_start(out=f_half[:], in_=channels[:, b, :])
+                f_raw.append(f_half)
             return f_raw
 
         def load_g(n, a):
@@ -79,54 +73,64 @@ def tile_head_v_kernel(tc, f0, f1, f2, w0, b0, w1, b1, w2, b2, anchors, y0, grad
 
         sig = const.tile([P, PACK, P], F32)
         nc.scalar.activation(out=sig[:], in_=y_sb[:].rearrange("q (p r) -> q r p", r=PACK), func=ACT.Sigmoid)
-        slope = const.tile([P, PACK, P], F32)
+        slope_xy = const.tile([P, PACK, P], F32)
         nc.vector.scalar_tensor_tensor(
-            out=slope[:], in0=sig[:], scalar=1.0, in1=sig[:], op0=ALU.subtract, op1=ALU.mult
+            out=slope_xy[:], in0=sig[:], scalar=1.0, in1=sig[:], op0=ALU.subtract, op1=ALU.mult
         )
+        slope_wh = const.tile([P, PACK, P], F32)
         nc.vector.scalar_tensor_tensor(
-            out=slope[P // 2 : P], in0=slope[P // 2 : P], scalar=-8.0, in1=sig[P // 2 : P], op0=ALU.mult, op1=ALU.mult
+            out=slope_wh[:], in0=slope_xy[:], scalar=-8.0, in1=sig[:], op0=ALU.mult, op1=ALU.mult
         )
-        slope_t = flip_banks.tile([P, PACK, P], F32, tag="flip")
+        xy_t = flip_banks.tile([P, PACK, B * NA, NS, HALVES], F32, tag="flip")
+        wh_t = flip_banks.tile([P, PACK, B * NA, NS, HALVES], F32, tag="flip")
         for r in range(PACK):
-            nc.tensor.transpose(out=slope_t[:, r, :], in_=slope[:, r, :], identity=ident[:])
-        factor = const.tile([P, PACK, NS, HALVES, B, NA], F32)
-        plain = P // 2
+            nc.tensor.transpose(
+                out=xy_t[:, r].rearrange("p q j h -> p (q j h)"), in_=slope_xy[:, r, :], identity=ident[:]
+            )
+        for r in range(PACK):
+            nc.tensor.transpose(
+                out=wh_t[:, r].rearrange("p q j h -> p (q j h)"), in_=slope_wh[:, r, :], identity=ident[:]
+            )
+        factor = const.tile([P, PACK, B * NA, NS, HALVES], F32)
         nc.vector.tensor_scalar(
-            out=factor[:].rearrange("p r j h n a -> p r (j h n a)")[:, :, 0:plain],
-            in0=slope_t[:, :, 0:plain],
+            out=factor[:, :, :, 0:2, :].rearrange("p r q j h -> p r q (j h)"),
+            in0=xy_t[:, :, :, 0:2, :].rearrange("p r q j h -> p r q (j h)"),
             scalar1=-2.0,
             scalar2=None,
             op0=ALU.mult,
         )
-        per_field = HALVES * B * NA
         for w in range(2):
             nc.vector.tensor_tensor(
-                out=factor[:, :, 2 + w].rearrange("p r h n a -> p r (h n) a"),
-                in0=slope_t[:, :, plain + w * per_field : plain + (w + 1) * per_field].rearrange(
-                    "p r (x a) -> p r x a", a=NA
-                ),
+                out=factor[:, :, :, 2 + w, :].rearrange("p r (n a) h -> p (r n) a h", a=NA),
+                in0=wh_t[:, :, :, 2 + w, :].rearrange("p r (n a) h -> p (r n) a h", a=NA),
                 in1=anc[:]
                 .rearrange("p (a w) -> p w a", w=2)[:, w, :]
                 .unsqueeze(1)
-                .unsqueeze(1)
-                .to_broadcast([P, PACK, HALVES * B, NA]),
+                .unsqueeze(3)
+                .to_broadcast([P, PACK * B, NA, HALVES]),
                 op=ALU.mult,
             )
 
-        def quantise_f(n, h):
-            words = f_raws[n][:].bitcast(F32).rearrange(
-                "c (i h p s) -> c i h s p", i=C_PER_PART, h=HALVES, p=P, s=2
-            )
-            f_grouped = f_pass.tile([P, C * PACK], BF16, align_bytes=64)
-            grouped_words = f_grouped[:].bitcast(F32).rearrange("p (c b x) -> p b c x", b=2, x=4)
+        def flip_f(n):
+            f_grouped = f_image.tile([P, HALVES, C * PACK], BF16, align_bytes=64)
+            grouped_words = f_grouped[:].bitcast(F32).rearrange("p h (c b x) -> p h b c x", b=2, x=4)
             for b in range(2):
-                flip = flip_banks.tile([P, 4, P], F32, tag="flip")
-                for x in range(4):
-                    nc.tensor.transpose(out=flip[:, x, :], in_=words[:, 2 * b + x // 2, h, x % 2, :], identity=ident[:])
-                nc.scalar.copy(out=grouped_words[:, b], in_=flip[:].rearrange("p x c -> p c x"))
-            f_codes = f_pass.tile([P, C], U32, align_bytes=64)
-            f_scales = f_pass.tile([P, C], U8, align_bytes=64)
-            nc.vector.quantize_mx(out=f_codes[:].bitcast(E4M3_X4), scales=f_scales[:], in_=f_grouped[:])
+                words = f_raws[n][b][:].bitcast(F32).rearrange("c (i h p s) -> c i h s p", i=2, h=HALVES, p=P, s=2)
+                for h in range(HALVES):
+                    flip = flip_banks.tile([P, 4, P], F32, tag="flip")
+                    for x in range(4):
+                        nc.tensor.transpose(out=flip[:, x, :], in_=words[:, x // 2, h, x % 2, :], identity=ident[:])
+                    nc.scalar.copy(out=grouped_words[:, h, b], in_=flip[:].rearrange("p x c -> p c x"))
+            return f_grouped
+
+        def quantise_f(f_grouped):
+            f_codes = f_image.tile([P, HALVES, C], U32, align_bytes=64)
+            f_scales = f_image.tile([P, HALVES, C], U8, align_bytes=64)
+            nc.vector.quantize_mx(
+                out=f_codes[:].rearrange("p h c -> p (h c)").bitcast(E4M3_X4),
+                scales=f_scales[:].rearrange("p h c -> p (h c)"),
+                in_=f_grouped[:].rearrange("p h k -> p (h k)"),
+            )
             return f_codes, f_scales
 
         def quantise_dy(n, a):
@@ -136,7 +140,7 @@ def tile_head_v_kernel(tc, f0, f1, f2, w0, b0, w1, b1, w2, b2, anchors, y0, grad
             nc.vector.tensor_tensor(
                 out=dy[:, :, 0:NS, :],
                 in0=dy[:, :, 0:NS, :],
-                in1=factor[:, :, :, :, n, a].rearrange("p r j h -> p h j r"),
+                in1=factor[:, :, n * NA + a].rearrange("p r j h -> p h j r"),
                 op=ALU.mult,
             )
             dy_codes = g_piece.tile([P, HALVES * NO], U32, align_bytes=64)
@@ -147,21 +151,21 @@ def tile_head_v_kernel(tc, f0, f1, f2, w0, b0, w1, b1, w2, b2, anchors, y0, grad
             return dy_codes, dy_scales
 
         acc = [acc_banks.tile([P, C], F32, name="acc%d" % a) for a in range(NA)]
-        f_mx = [[quantise_f(0, h) for h in range(HALVES)]]
+        f_mx = [quantise_f(flip_f(0))]
         for n in range(B):
             if n + 1 < B:
-                f_mx.append([quantise_f(n + 1, h) for h in range(HALVES)])
+                f_next = flip_f(n + 1)
+            f_codes, f_scales = f_mx[n]
             for a in range(NA):
                 dy_codes, dy_scales = quantise_dy(n, a)
                 for h in range(HALVES):
-                    f_codes, f_scales = f_mx[n][h]
                     fields = slice(h * NO, (h + 1) * NO)
                     nc.tensor.matmul_mx(
                         out=acc[a][:],
                         lhsT=dy_codes[:, fields].bitcast(E5M2_X4),
                         lhsT_scale=dy_scales[:, fields],
-                        rhs=f_codes[:].bitcast(E4M3_X4),
-                        rhs_scale=f_scales[:],
+                        rhs=f_codes[:, h, :].bitcast(E4M3_X4),
+                        rhs_scale=f_scales[:, h, :],
                         start=(n == 0 and h == 0),
                         stop=(n == B - 1 and h == HALVES - 1),
                     )
@@ -169,3 +173,5 @@ def tile_head_v_kernel(tc, f0, f1, f2, w0, b0, w1, b1, w2, b2, anchors, y0, grad
                     rows = result.tile([P, C], F32)
                     nc.scalar.copy(out=rows[:], in_=acc[a][:])
                     nc.sync.dma_start(out=out[a * NO : (a + 1) * NO, :], in_=rows[:])
+            if n + 1 < B:
+                f_mx.append(quantise_f(f_next))

@@ -22,6 +22,8 @@ HALVES = MAP // K_PASS
 NA = 4
 NO = 128
 NS = 4
+FLIP_BANKS = 4
+VECTOR_FIELDS = 80
 
 FLOPS = 2 * B * MAP * NA * NO * C
 BYTES = 2 * B * C * MAP + 2 * B * NA * MAP * NO + 4 * B * NA * NS * MAP + 2 * NA * 2 + 4 * NA * NO * C
@@ -32,11 +34,12 @@ def tile_head_v_kernel(tc, f0, f1, f2, w0, b0, w1, b1, w2, b2, anchors, y0, grad
     with ExitStack() as ctx:
         const = ctx.enter_context(tc.tile_pool(name="const", bufs=1))
         f_load = ctx.enter_context(tc.tile_pool(name="f_load", bufs=B * 2))
-        f_image = ctx.enter_context(tc.tile_pool(name="f_image", bufs=B))
+        f_pass = ctx.enter_context(tc.tile_pool(name="f_pass", bufs=B * HALVES))
         g_piece = ctx.enter_context(tc.tile_pool(name="g_piece", bufs=B * NA))
         result = ctx.enter_context(tc.tile_pool(name="result", bufs=NA))
         acc_banks = ctx.enter_context(tc.psum_pool(name="acc_banks", bufs=1))
-        flip_banks = ctx.enter_context(tc.psum_pool(name="flip_banks", bufs=4))
+        flip_banks = ctx.enter_context(tc.psum_pool(name="flip_banks", bufs=FLIP_BANKS))
+        ctx.enter_context(tc.manual_schedule())
 
         ident = const.tile([P, P], F32)
         masks.make_identity(nc, ident[:])
@@ -71,6 +74,52 @@ def tile_head_v_kernel(tc, f0, f1, f2, w0, b0, w1, b1, w2, b2, anchors, y0, grad
                 f_raws.append(load_f(n + 1))
             g_raws.append([load_g(n, a) for a in range(NA)])
 
+        def flip_f(n):
+            flips = []
+            for h in range(HALVES):
+                for b in range(2):
+                    words = f_raws[n][b][:].bitcast(F32).rearrange(
+                        "c (i h p s) -> c i h s p", i=2, h=HALVES, p=P, s=2
+                    )
+                    flip = flip_banks.tile([P, 4, P], F32, tag="flip")
+                    for x in range(4):
+                        nc.tensor.transpose(out=flip[:, x, :], in_=words[:, x // 2, h, x % 2, :], identity=ident[:])
+                    flips.append(flip)
+            return flips
+
+        def gather_f(f_grouped, b, flip):
+            grouped_words = f_grouped[:].bitcast(F32).rearrange("p (c b x) -> p b c x", b=2, x=4)
+            nc.scalar.copy(out=grouped_words[:, b], in_=flip[:].rearrange("p x c -> p c x"))
+
+        def quantise_f(f_grouped):
+            f_codes = f_pass.tile([P, C], U32, align_bytes=64)
+            f_scales = f_pass.tile([P, C], U8, align_bytes=64)
+            nc.vector.quantize_mx(out=f_codes[:].bitcast(E4M3_X4), scales=f_scales[:], in_=f_grouped[:])
+            return f_codes, f_scales
+
+        def regroup_dy(n, a):
+            dy = g_piece.tile([P, HALVES, NO, PACK], BF16, align_bytes=64)
+            by_field = g_raws[n][a][:].rearrange("p h r j -> p h j r")
+            nc.vector.tensor_copy(out=dy[:, :, 0:VECTOR_FIELDS, :], in_=by_field[:, :, 0:VECTOR_FIELDS, :])
+            nc.scalar.copy(out=dy[:, :, VECTOR_FIELDS:NO, :], in_=by_field[:, :, VECTOR_FIELDS:NO, :])
+            return dy
+
+        def apply_factor(dy, n, a):
+            nc.vector.tensor_tensor(
+                out=dy[:, :, 0:NS, :],
+                in0=dy[:, :, 0:NS, :],
+                in1=factor[:, :, n * NA + a].rearrange("p r j h -> p h j r"),
+                op=ALU.mult,
+            )
+
+        def quantise_dy(dy):
+            dy_codes = g_piece.tile([P, HALVES * NO], U32, align_bytes=64)
+            dy_scales = g_piece.tile([P, HALVES * NO], U8, align_bytes=64)
+            nc.vector.quantize_mx(
+                out=dy_codes[:].bitcast(E5M2_X4), scales=dy_scales[:], in_=dy[:].rearrange("p h j r -> p (h j r)")
+            )
+            return dy_codes, dy_scales
+
         sig = const.tile([P, PACK, P], F32)
         nc.scalar.activation(out=sig[:], in_=y_sb[:].rearrange("q (p r) -> q r p", r=PACK), func=ACT.Sigmoid)
         slope_xy = const.tile([P, PACK, P], F32)
@@ -81,6 +130,15 @@ def tile_head_v_kernel(tc, f0, f1, f2, w0, b0, w1, b1, w2, b2, anchors, y0, grad
         nc.vector.scalar_tensor_tensor(
             out=slope_wh[:], in0=slope_xy[:], scalar=-8.0, in1=sig[:], op0=ALU.mult, op1=ALU.mult
         )
+
+        f_mx = []
+        flips = flip_f(0)
+        for h in range(HALVES):
+            f_grouped = f_pass.tile([P, C * PACK], BF16, align_bytes=64)
+            for b in range(2):
+                gather_f(f_grouped, b, flips[2 * h + b])
+            f_mx.append(quantise_f(f_grouped))
+
         xy_t = flip_banks.tile([P, PACK, B * NA, NS, HALVES], F32, tag="flip")
         wh_t = flip_banks.tile([P, PACK, B * NA, NS, HALVES], F32, tag="flip")
         for r in range(PACK):
@@ -111,67 +169,42 @@ def tile_head_v_kernel(tc, f0, f1, f2, w0, b0, w1, b1, w2, b2, anchors, y0, grad
                 op=ALU.mult,
             )
 
-        def flip_f(n):
-            f_grouped = f_image.tile([P, HALVES, C * PACK], BF16, align_bytes=64)
-            grouped_words = f_grouped[:].bitcast(F32).rearrange("p h (c b x) -> p h b c x", b=2, x=4)
-            for b in range(2):
-                words = f_raws[n][b][:].bitcast(F32).rearrange("c (i h p s) -> c i h s p", i=2, h=HALVES, p=P, s=2)
-                for h in range(HALVES):
-                    flip = flip_banks.tile([P, 4, P], F32, tag="flip")
-                    for x in range(4):
-                        nc.tensor.transpose(out=flip[:, x, :], in_=words[:, x // 2, h, x % 2, :], identity=ident[:])
-                    nc.scalar.copy(out=grouped_words[:, h, b], in_=flip[:].rearrange("p x c -> p c x"))
-            return f_grouped
-
-        def quantise_f(f_grouped):
-            f_codes = f_image.tile([P, HALVES, C], U32, align_bytes=64)
-            f_scales = f_image.tile([P, HALVES, C], U8, align_bytes=64)
-            nc.vector.quantize_mx(
-                out=f_codes[:].rearrange("p h c -> p (h c)").bitcast(E4M3_X4),
-                scales=f_scales[:].rearrange("p h c -> p (h c)"),
-                in_=f_grouped[:].rearrange("p h k -> p (h k)"),
-            )
-            return f_codes, f_scales
-
-        def quantise_dy(n, a):
-            dy = g_piece.tile([P, HALVES, NO, PACK], BF16, align_bytes=64)
-            copier = nc.scalar.copy if a == 0 else nc.vector.tensor_copy
-            copier(out=dy[:], in_=g_raws[n][a][:].rearrange("p h r j -> p h j r"))
-            nc.vector.tensor_tensor(
-                out=dy[:, :, 0:NS, :],
-                in0=dy[:, :, 0:NS, :],
-                in1=factor[:, :, n * NA + a].rearrange("p r j h -> p h j r"),
-                op=ALU.mult,
-            )
-            dy_codes = g_piece.tile([P, HALVES * NO], U32, align_bytes=64)
-            dy_scales = g_piece.tile([P, HALVES * NO], U8, align_bytes=64)
-            nc.vector.quantize_mx(
-                out=dy_codes[:].bitcast(E5M2_X4), scales=dy_scales[:], in_=dy[:].rearrange("p h j r -> p (h j r)")
-            )
-            return dy_codes, dy_scales
-
         acc = [acc_banks.tile([P, C], F32, name="acc%d" % a) for a in range(NA)]
-        f_mx = [quantise_f(flip_f(0))]
-        for n in range(B):
-            if n + 1 < B:
-                f_next = flip_f(n + 1)
-            f_codes, f_scales = f_mx[n]
-            for a in range(NA):
-                dy_codes, dy_scales = quantise_dy(n, a)
-                for h in range(HALVES):
-                    fields = slice(h * NO, (h + 1) * NO)
-                    nc.tensor.matmul_mx(
-                        out=acc[a][:],
-                        lhsT=dy_codes[:, fields].bitcast(E5M2_X4),
-                        lhsT_scale=dy_scales[:, fields],
-                        rhs=f_codes[:, h, :].bitcast(E4M3_X4),
-                        rhs_scale=f_scales[:, h, :],
-                        start=(n == 0 and h == 0),
-                        stop=(n == B - 1 and h == HALVES - 1),
-                    )
-                if n == B - 1:
-                    rows = result.tile([P, C], F32)
-                    nc.scalar.copy(out=rows[:], in_=acc[a][:])
-                    nc.sync.dma_start(out=out[a * NO : (a + 1) * NO, :], in_=rows[:])
-            if n + 1 < B:
-                f_mx.append(quantise_f(f_next))
+        pieces = [(n, a) for n in range(B) for a in range(NA)]
+        dy = regroup_dy(0, 0)
+        apply_factor(dy, 0, 0)
+        for i, (n, a) in enumerate(pieces):
+            more_f = n + 1 < B
+            more_dy = i + 1 < len(pieces)
+            if more_f and a == 0:
+                flips = flip_f(n + 1)
+            if more_f and a % 2 == 0:
+                f_grouped = f_pass.tile([P, C * PACK], BF16, align_bytes=64)
+            if more_f:
+                gather_f(f_grouped, a % 2, flips[a])
+            if more_dy:
+                dy_next = regroup_dy(*pieces[i + 1])
+            dy_codes, dy_scales = quantise_dy(dy)
+            if more_dy:
+                apply_factor(dy_next, *pieces[i + 1])
+                dy = dy_next
+            if more_f and a % 2 == 1:
+                f_mx.append(quantise_f(f_grouped))
+            for h in range(HALVES):
+                f_codes, f_scales = f_mx[HALVES * n + h]
+                fields = slice(h * NO, (h + 1) * NO)
+                nc.tensor.matmul_mx(
+                    out=acc[a][:],
+                    lhsT=dy_codes[:, fields].bitcast(E5M2_X4),
+                    lhsT_scale=dy_scales[:, fields],
+                    rhs=f_codes[:].bitcast(E4M3_X4),
+                    rhs_scale=f_scales[:],
+                    start=(n == 0 and h == 0),
+                    stop=(n == B - 1 and h == HALVES - 1),
+                )
+
+        for a in range(NA):
+            rows = result.tile([P, C], F32)
+            copier = nc.scalar.copy if a % 2 == 0 else nc.vector.tensor_copy
+            copier(out=rows[:], in_=acc[a][:])
+            nc.sync.dma_start(out=out[a * NO : (a + 1) * NO, :], in_=rows[:])

@@ -99,9 +99,15 @@ def tile_head_v_kernel(tc, f0, f1, f2, w0, b0, w1, b1, w2, b2, anchors, y0, grad
 
         def regroup_dy(n, a):
             dy = g_piece.tile([P, HALVES, NO, PACK], BF16, align_bytes=64)
-            by_field = g_raws[n][a][:].rearrange("p h r j -> p h j r")
-            nc.vector.tensor_copy(out=dy[:, :, 0:VECTOR_FIELDS, :], in_=by_field[:, :, 0:VECTOR_FIELDS, :])
-            nc.scalar.copy(out=dy[:, :, VECTOR_FIELDS:NO, :], in_=by_field[:, :, VECTOR_FIELDS:NO, :])
+            g_raw = g_raws[n][a]
+            nc.scalar.copy(
+                out=dy[:, :, VECTOR_FIELDS:NO, :],
+                in_=g_raw[:, :, :, VECTOR_FIELDS:NO].rearrange("p h r j -> p h j r"),
+            )
+            nc.vector.tensor_copy(
+                out=dy[:, :, 0:VECTOR_FIELDS, :].rearrange("p h (c i) r -> p h c r i", i=4),
+                in_=g_raw[:, :, :, 0:VECTOR_FIELDS].rearrange("p h r (c i) -> p h c r i", i=4),
+            )
             return dy
 
         def apply_factor(dy, n, a):
@@ -131,13 +137,14 @@ def tile_head_v_kernel(tc, f0, f1, f2, w0, b0, w1, b1, w2, b2, anchors, y0, grad
             out=slope_wh[:], in0=slope_xy[:], scalar=-8.0, in1=sig[:], op0=ALU.mult, op1=ALU.mult
         )
 
-        f_mx = []
         flips = flip_f(0)
+        f_groupeds = []
         for h in range(HALVES):
-            f_grouped = f_pass.tile([P, C * PACK], BF16, align_bytes=64)
+            f_grouped = f_pass.tile([P, C * PACK], BF16, align_bytes=64, tag="f_grouped")
             for b in range(2):
                 gather_f(f_grouped, b, flips[2 * h + b])
-            f_mx.append(quantise_f(f_grouped))
+            f_groupeds.append(f_grouped)
+        f_mx = [quantise_f(f_groupeds[0])]
 
         xy_t = flip_banks.tile([P, PACK, B * NA, NS, HALVES], F32, tag="flip")
         wh_t = flip_banks.tile([P, PACK, B * NA, NS, HALVES], F32, tag="flip")
@@ -169,27 +176,11 @@ def tile_head_v_kernel(tc, f0, f1, f2, w0, b0, w1, b1, w2, b2, anchors, y0, grad
                 op=ALU.mult,
             )
 
+        f_mx.append(quantise_f(f_groupeds[1]))
+
         acc = [acc_banks.tile([P, C], F32, name="acc%d" % a) for a in range(NA)]
-        pieces = [(n, a) for n in range(B) for a in range(NA)]
-        dy = regroup_dy(0, 0)
-        apply_factor(dy, 0, 0)
-        for i, (n, a) in enumerate(pieces):
-            more_f = n + 1 < B
-            more_dy = i + 1 < len(pieces)
-            if more_f and a == 0:
-                flips = flip_f(n + 1)
-            if more_f and a % 2 == 0:
-                f_grouped = f_pass.tile([P, C * PACK], BF16, align_bytes=64)
-            if more_f:
-                gather_f(f_grouped, a % 2, flips[a])
-            if more_dy:
-                dy_next = regroup_dy(*pieces[i + 1])
-            dy_codes, dy_scales = quantise_dy(dy)
-            if more_dy:
-                apply_factor(dy_next, *pieces[i + 1])
-                dy = dy_next
-            if more_f and a % 2 == 1:
-                f_mx.append(quantise_f(f_grouped))
+
+        def multiply(n, a, dy_codes, dy_scales):
             for h in range(HALVES):
                 f_codes, f_scales = f_mx[HALVES * n + h]
                 fields = slice(h * NO, (h + 1) * NO)
@@ -203,8 +194,29 @@ def tile_head_v_kernel(tc, f0, f1, f2, w0, b0, w1, b1, w2, b2, anchors, y0, grad
                     stop=(n == B - 1 and h == HALVES - 1),
                 )
 
+        flips = flip_f(1)
+        for n in range(B):
+            more_f = n + 1 < B
+            dys = []
+            f_groupeds = []
+            for a in range(NA):
+                dys.append(regroup_dy(n, a))
+                if more_f and a % 2 == 0:
+                    f_groupeds.append(f_pass.tile([P, C * PACK], BF16, align_bytes=64, name="f_grouped", tag="f_grouped"))
+                if more_f:
+                    gather_f(f_groupeds[a // 2], a % 2, flips[a])
+                if a > 0:
+                    multiply(n, a - 1, *quantise_dy(dys[a - 1]))
+                apply_factor(dys[a], n, a)
+            if n + 2 < B:
+                flips = flip_f(n + 2)
+            if more_f:
+                f_mx.append(quantise_f(f_groupeds[0]))
+            multiply(n, NA - 1, *quantise_dy(dys[NA - 1]))
+            if more_f:
+                f_mx.append(quantise_f(f_groupeds[1]))
+
         for a in range(NA):
             rows = result.tile([P, C], F32)
-            copier = nc.scalar.copy if a % 2 == 0 else nc.vector.tensor_copy
-            copier(out=rows[:], in_=acc[a][:])
+            nc.scalar.copy(out=rows[:], in_=acc[a][:])
             nc.sync.dma_start(out=out[a * NO : (a + 1) * NO, :], in_=rows[:])

@@ -24,6 +24,8 @@ NO = 128
 NS = 4
 FLIP_BANKS = 4
 VECTOR_FIELDS = 80
+WARM_FREE = 5
+WARM_BEHIND_Y = 3
 
 FLOPS = 2 * B * MAP * NA * NO * C
 BYTES = 2 * B * C * MAP + 2 * B * NA * MAP * NO + 4 * B * NA * NS * MAP + 2 * NA * 2 + 4 * NA * NO * C
@@ -73,6 +75,12 @@ def tile_head_v_kernel(tc, f0, f1, f2, w0, b0, w1, b1, w2, b2, anchors, y0, grad
             if n + 1 < B:
                 f_raws.append(load_f(n + 1))
             g_raws.append([load_g(n, a) for a in range(NA)])
+
+        warm = acc_banks.tile([P, P], F32, name="warm", tag="acc3")
+        for i in range(WARM_FREE):
+            nc.tensor.matmul(out=warm[:], lhsT=ident[:], rhs=ident[:], start=True, stop=True)
+        for i in range(WARM_BEHIND_Y):
+            nc.tensor.matmul(out=warm[:], lhsT=ident[:], rhs=y_sb[:, 0:P], start=True, stop=True)
 
         def flip_f(n):
             flips = []
@@ -178,7 +186,7 @@ def tile_head_v_kernel(tc, f0, f1, f2, w0, b0, w1, b1, w2, b2, anchors, y0, grad
 
         f_mx.append(quantise_f(f_groupeds[1]))
 
-        acc = [acc_banks.tile([P, C], F32, name="acc%d" % a) for a in range(NA)]
+        acc = [acc_banks.tile([P, C], F32, name="acc%d" % a, tag="acc%d" % a) for a in range(NA)]
 
         def multiply(n, a, dy_codes, dy_scales):
             for h in range(HALVES):

@@ -24,6 +24,7 @@ NO = 128
 NS = 4
 FLIP_BANKS = 4
 VECTOR_FIELDS = 80
+VECTOR_FIELDS_LAST = 64
 WARM_FREE = 5
 WARM_BEHIND_Y = 3
 
@@ -108,13 +109,14 @@ def tile_head_v_kernel(tc, f0, f1, f2, w0, b0, w1, b1, w2, b2, anchors, y0, grad
         def regroup_dy(n, a):
             dy = g_piece.tile([P, HALVES, NO, PACK], BF16, align_bytes=64)
             g_raw = g_raws[n][a]
+            split = VECTOR_FIELDS if n + 1 < B else VECTOR_FIELDS_LAST
             nc.scalar.copy(
-                out=dy[:, :, VECTOR_FIELDS:NO, :],
-                in_=g_raw[:, :, :, VECTOR_FIELDS:NO].rearrange("p h r j -> p h j r"),
+                out=dy[:, :, split:NO, :],
+                in_=g_raw[:, :, :, split:NO].rearrange("p h r j -> p h j r"),
             )
             nc.vector.tensor_copy(
-                out=dy[:, :, 0:VECTOR_FIELDS, :].rearrange("p h (c i) r -> p h c r i", i=4),
-                in_=g_raw[:, :, :, 0:VECTOR_FIELDS].rearrange("p h r (c i) -> p h c r i", i=4),
+                out=dy[:, :, 0:split, :].rearrange("p h (c i) r -> p h c r i", i=4),
+                in_=g_raw[:, :, :, 0:split].rearrange("p h r (c i) -> p h c r i", i=4),
             )
             return dy
 
@@ -224,7 +226,13 @@ def tile_head_v_kernel(tc, f0, f1, f2, w0, b0, w1, b1, w2, b2, anchors, y0, grad
             if more_f:
                 f_mx.append(quantise_f(f_groupeds[1]))
 
-        for a in range(NA):
+        for a in range(NA - 1):
             rows = result.tile([P, C], F32)
             nc.scalar.copy(out=rows[:], in_=acc[a][:])
             nc.sync.dma_start(out=out[a * NO : (a + 1) * NO, :], in_=rows[:])
+        a = NA - 1
+        for part in range(2):
+            cols = slice(part * (C // 2), (part + 1) * (C // 2))
+            rows_half = result.tile([P, C // 2], F32)
+            nc.scalar.copy(out=rows_half[:], in_=acc[a][:, cols])
+            nc.sync.dma_start(out=out[a * NO : (a + 1) * NO, cols], in_=rows_half[:])

@@ -111,8 +111,8 @@ def tile_head_v_kernel(tc, f0, f1, f2, w0, b0, w1, b1, w2, b2, anchors, y0, grad
             g_raw = g_raws[n][a]
             split = VECTOR_FIELDS if n + 1 < B else VECTOR_FIELDS_LAST
             nc.scalar.copy(
-                out=dy[:, :, split:NO, :],
-                in_=g_raw[:, :, :, split:NO].rearrange("p h r j -> p h j r"),
+                out=dy[:, :, split:NO, :].rearrange("p h (c i) r -> p h c r i", i=4),
+                in_=g_raw[:, :, :, split:NO].rearrange("p h r (c i) -> p h c r i", i=4),
             )
             nc.vector.tensor_copy(
                 out=dy[:, :, 0:split, :].rearrange("p h (c i) r -> p h c r i", i=4),

@@ -27,6 +27,7 @@ VECTOR_FIELDS = 80
 VECTOR_FIELDS_LAST = 64
 WARM_FREE = 5
 WARM_BEHIND_Y = 3
+PAIR = 2
 
 FLOPS = 2 * B * MAP * NA * NO * C
 BYTES = 2 * B * C * MAP + 2 * B * NA * MAP * NO + 4 * B * NA * NS * MAP + 2 * NA * 2 + 4 * NA * NO * C
@@ -38,7 +39,8 @@ def tile_head_v_kernel(tc, f0, f1, f2, w0, b0, w1, b1, w2, b2, anchors, y0, grad
         const = ctx.enter_context(tc.tile_pool(name="const", bufs=1))
         f_load = ctx.enter_context(tc.tile_pool(name="f_load", bufs=B * 2))
         f_pass = ctx.enter_context(tc.tile_pool(name="f_pass", bufs=B * HALVES))
-        g_piece = ctx.enter_context(tc.tile_pool(name="g_piece", bufs=B * NA))
+        g_piece = ctx.enter_context(tc.tile_pool(name="g_piece", bufs=B * NA // PAIR))
+        codes = ctx.enter_context(tc.tile_pool(name="codes", bufs=B * NA))
         result = ctx.enter_context(tc.tile_pool(name="result", bufs=NA))
         acc_banks = ctx.enter_context(tc.psum_pool(name="acc_banks", bufs=1))
         flip_banks = ctx.enter_context(tc.psum_pool(name="flip_banks", bufs=FLIP_BANKS))
@@ -62,20 +64,27 @@ def tile_head_v_kernel(tc, f0, f1, f2, w0, b0, w1, b1, w2, b2, anchors, y0, grad
                 f_raw.append(f_half)
             return f_raw
 
+        g_raws = [
+            [
+                g_piece.tile([P, PAIR * HALVES, PACK, NO], BF16, name="g_raw", tag="g_raw")
+                for u in range(NA // PAIR)
+            ]
+            for n in range(B)
+        ]
+
         def load_g(n, a):
-            g_raw = g_piece.tile([P, HALVES, PACK, NO], BF16)
+            mine = slice((a % PAIR) * HALVES, (a % PAIR + 1) * HALVES)
             nc.sync.dma_start(
-                out=g_raw[:].rearrange("p h r j -> p h (r j)"),
+                out=g_raws[n][a // PAIR][:, mine].rearrange("p h r j -> p h (r j)"),
                 in_=grad_out[n, a * MAP : (a + 1) * MAP, :].rearrange("(h p r) j -> p h (r j)", h=HALVES, r=PACK),
             )
-            return g_raw
 
-        f_raws = [load_f(0)]
-        g_raws = []
+        f_raws = [load_f(0), load_f(1)]
         for n in range(B):
-            if n + 1 < B:
-                f_raws.append(load_f(n + 1))
-            g_raws.append([load_g(n, a) for a in range(NA)])
+            for a in range(NA):
+                load_g(n, a)
+                if a == PAIR - 1 and 1 <= n < B - 1:
+                    f_raws.append(load_f(n + 1))
 
         warm = acc_banks.tile([P, P], F32, name="warm", tag="acc3")
         for i in range(WARM_FREE):
@@ -106,33 +115,35 @@ def tile_head_v_kernel(tc, f0, f1, f2, w0, b0, w1, b1, w2, b2, anchors, y0, grad
             nc.vector.quantize_mx(out=f_codes[:].bitcast(E4M3_X4), scales=f_scales[:], in_=f_grouped[:])
             return f_codes, f_scales
 
-        def regroup_dy(n, a):
-            dy = g_piece.tile([P, HALVES, NO, PACK], BF16, align_bytes=64)
-            g_raw = g_raws[n][a]
+        def regroup_dy(dy, n, a):
+            g_raw = g_raws[n][a // PAIR]
+            mine = slice((a % PAIR) * HALVES, (a % PAIR + 1) * HALVES)
             split = VECTOR_FIELDS if n + 1 < B else VECTOR_FIELDS_LAST
             nc.scalar.copy(
-                out=dy[:, :, split:NO, :].rearrange("p h (c i) r -> p h c r i", i=4),
-                in_=g_raw[:, :, :, split:NO].rearrange("p h r (c i) -> p h c r i", i=4),
+                out=dy[:, mine, split:NO, :].rearrange("p h (c i) r -> p h c r i", i=4),
+                in_=g_raw[:, mine, :, split:NO].rearrange("p h r (c i) -> p h c r i", i=4),
             )
             nc.vector.tensor_copy(
-                out=dy[:, :, 0:split, :].rearrange("p h (c i) r -> p h c r i", i=4),
-                in_=g_raw[:, :, :, 0:split].rearrange("p h r (c i) -> p h c r i", i=4),
+                out=dy[:, mine, NS:split, :].rearrange("p h (c i) r -> p h c r i", i=4),
+                in_=g_raw[:, mine, :, NS:split].rearrange("p h r (c i) -> p h c r i", i=4),
             )
-            return dy
 
-        def apply_factor(dy, n, a):
+        def apply_factor(dy, n, u):
+            mine = slice(u * PAIR * HALVES, (u + 1) * PAIR * HALVES)
             nc.vector.tensor_tensor(
                 out=dy[:, :, 0:NS, :],
-                in0=dy[:, :, 0:NS, :],
-                in1=factor[:, :, n * NA + a].rearrange("p r j h -> p h j r"),
+                in0=g_raws[n][u][:, :, :, 0:NS].rearrange("p g r j -> p g j r"),
+                in1=factor[:].rearrange("p j r (n a) h -> p n (a h) j r", n=B)[:, n, mine],
                 op=ALU.mult,
             )
 
-        def quantise_dy(dy):
-            dy_codes = g_piece.tile([P, HALVES * NO], U32, align_bytes=64)
-            dy_scales = g_piece.tile([P, HALVES * NO], U8, align_bytes=64)
+        def quantise_dy(dy, first, count):
+            dy_codes = codes.tile([P, count * NO], U32, align_bytes=64, name="dy_codes", tag="dy_codes")
+            dy_scales = codes.tile([P, count * NO], U8, align_bytes=64, name="dy_scales", tag="dy_scales")
             nc.vector.quantize_mx(
-                out=dy_codes[:].bitcast(E5M2_X4), scales=dy_scales[:], in_=dy[:].rearrange("p h j r -> p (h j r)")
+                out=dy_codes[:].bitcast(E5M2_X4),
+                scales=dy_scales[:],
+                in_=dy[:, first : first + count].rearrange("p g j r -> p (g j r)"),
             )
             return dy_codes, dy_scales
 
@@ -166,17 +177,14 @@ def tile_head_v_kernel(tc, f0, f1, f2, w0, b0, w1, b1, w2, b2, anchors, y0, grad
             nc.tensor.transpose(
                 out=wh_t[:, r].rearrange("p q j h -> p (q j h)"), in_=slope_wh[:, r, :], identity=ident[:]
             )
-        factor = const.tile([P, PACK, B * NA, NS, HALVES], F32)
-        nc.vector.tensor_scalar(
-            out=factor[:, :, :, 0:2, :].rearrange("p r q j h -> p r q (j h)"),
-            in0=xy_t[:, :, :, 0:2, :].rearrange("p r q j h -> p r q (j h)"),
-            scalar1=-2.0,
-            scalar2=None,
-            op0=ALU.mult,
-        )
+        factor = const.tile([P, NS, PACK, B * NA, HALVES], F32)
+        for j in range(2):
+            nc.vector.tensor_scalar(
+                out=factor[:, j], in0=xy_t[:, :, :, j, :], scalar1=-2.0, scalar2=None, op0=ALU.mult
+            )
         for w in range(2):
             nc.vector.tensor_tensor(
-                out=factor[:, :, :, 2 + w, :].rearrange("p r (n a) h -> p (r n) a h", a=NA),
+                out=factor[:, 2 + w].rearrange("p r (n a) h -> p (r n) a h", a=NA),
                 in0=wh_t[:, :, :, 2 + w, :].rearrange("p r (n a) h -> p (r n) a h", a=NA),
                 in1=anc[:]
                 .rearrange("p (a w) -> p w a", w=2)[:, w, :]
@@ -190,7 +198,8 @@ def tile_head_v_kernel(tc, f0, f1, f2, w0, b0, w1, b1, w2, b2, anchors, y0, grad
 
         acc = [acc_banks.tile([P, C], F32, name="acc%d" % a, tag="acc%d" % a) for a in range(NA)]
 
-        def multiply(n, a, dy_codes, dy_scales):
+        def finish(n, a, dy):
+            dy_codes, dy_scales = quantise_dy(dy, (a % PAIR) * HALVES, HALVES)
             for h in range(HALVES):
                 f_codes, f_scales = f_mx[HALVES * n + h]
                 fields = slice(h * NO, (h + 1) * NO)
@@ -210,19 +219,24 @@ def tile_head_v_kernel(tc, f0, f1, f2, w0, b0, w1, b1, w2, b2, anchors, y0, grad
             dys = []
             f_groupeds = []
             for a in range(NA):
-                dys.append(regroup_dy(n, a))
+                if a % PAIR == 0:
+                    dys.append(g_piece.tile([P, PAIR * HALVES, NO, PACK], BF16, align_bytes=64, name="dy", tag="dy"))
+                regroup_dy(dys[a // PAIR], n, a)
                 if more_f and a % 2 == 0:
                     f_groupeds.append(f_pass.tile([P, C * PACK], BF16, align_bytes=64, name="f_grouped", tag="f_grouped"))
                 if more_f:
                     gather_f(f_groupeds[a // 2], a % 2, flips[a])
+                if a == 0:
+                    apply_factor(dys[0], n, 0)
                 if a > 0:
-                    multiply(n, a - 1, *quantise_dy(dys[a - 1]))
-                apply_factor(dys[a], n, a)
+                    finish(n, a - 1, dys[(a - 1) // PAIR])
+                if a == 2:
+                    apply_factor(dys[1], n, 1)
             if n + 2 < B:
                 flips = flip_f(n + 2)
             if more_f:
                 f_mx.append(quantise_f(f_groupeds[0]))
-            multiply(n, NA - 1, *quantise_dy(dys[NA - 1]))
+            finish(n, NA - 1, dys[1])
             if more_f:
                 f_mx.append(quantise_f(f_groupeds[1]))
 

from contextlib import ExitStack

import concourse.masks as masks
import concourse.mybir as mybir

F32 = mybir.dt.float32
BF16 = mybir.dt.bfloat16
U32 = mybir.dt.uint32
U8 = mybir.dt.uint8
E4M3_X4 = mybir.dt.float8_e4m3fn_x4
E5M2_X4 = mybir.dt.float8_e5m2_x4
ALU = mybir.AluOpType
ACT = mybir.ActivationFunctionType

P = 128
PACK = 4
K_PASS = P * PACK
B = 4
C = 512
MAP = 32 * 32
HALVES = MAP // K_PASS
NA = 4
NO = 128
NS = 4
FLIP_BANKS = 4
VECTOR_FIELDS = 80
VECTOR_FIELDS_LAST = 64
WARM_FREE = 5
WARM_BEHIND_Y = 3
PAIR = 2

FLOPS = 2 * B * MAP * NA * NO * C
BYTES = 2 * B * C * MAP + 2 * B * NA * MAP * NO + 4 * B * NA * NS * MAP + 2 * NA * 2 + 4 * NA * NO * C


def tile_head_v_kernel(tc, f0, f1, f2, w0, b0, w1, b1, w2, b2, anchors, y0, grad_out, out):
    nc = tc.nc
    with ExitStack() as ctx:
        const = ctx.enter_context(tc.tile_pool(name="const", bufs=1))
        f_load = ctx.enter_context(tc.tile_pool(name="f_load", bufs=B * 2))
        f_pass = ctx.enter_context(tc.tile_pool(name="f_pass", bufs=B * HALVES))
        g_piece = ctx.enter_context(tc.tile_pool(name="g_piece", bufs=B * NA // PAIR))
        codes = ctx.enter_context(tc.tile_pool(name="codes", bufs=B * NA))
        result = ctx.enter_context(tc.tile_pool(name="result", bufs=NA))
        acc_banks = ctx.enter_context(tc.psum_pool(name="acc_banks", bufs=1))
        flip_banks = ctx.enter_context(tc.psum_pool(name="flip_banks", bufs=FLIP_BANKS))
        ctx.enter_context(tc.manual_schedule())

        ident = const.tile([P, P], F32)
        masks.make_identity(nc, ident[:])

        y_rows = y0.rearrange("n (a j) u v -> (n a) j (u v)", j=NO)[:, 0:NS, :]
        y_sb = const.tile([P, K_PASS], F32)
        nc.sync.dma_start(out=y_sb[:], in_=y_rows.rearrange("q j (h k) -> q (j h) k", h=HALVES))
        anc = const.tile([P, NA * 2], BF16)
        nc.scalar.dma_start(out=anc[:], in_=anchors[0].rearrange("a w -> (a w)").partition_broadcast(P))

        def load_f(n):
            channels = f0[n].rearrange("(p b i) u v -> p b (i u v)", b=2, i=2)
            f_raw = []
            for b in range(2):
                f_half = f_load.tile([P, 2 * MAP], BF16)
                nc.sync.dma_start(out=f_half[:], in_=channels[:, b, :])
                f_raw.append(f_half)
            return f_raw

        g_raws = [
            [
                g_piece.tile([P, PAIR * HALVES, PACK, NO], BF16, name="g_raw", tag="g_raw")
                for u in range(NA // PAIR)
            ]
            for n in range(B)
        ]

        def load_g(n, a):
            mine = slice((a % PAIR) * HALVES, (a % PAIR + 1) * HALVES)
            nc.sync.dma_start(
                out=g_raws[n][a // PAIR][:, mine].rearrange("p h r j -> p h (r j)"),
                in_=grad_out[n, a * MAP : (a + 1) * MAP, :].rearrange("(h p r) j -> p h (r j)", h=HALVES, r=PACK),
            )

        f_raws = [load_f(0), load_f(1)]
        for n in range(B):
            for a in range(NA):
                load_g(n, a)
                if a == PAIR - 1 and 1 <= n < B - 1:
                    f_raws.append(load_f(n + 1))

        warm = acc_banks.tile([P, P], F32, name="warm", tag="acc3")
        for i in range(WARM_FREE):
            nc.tensor.matmul(out=warm[:], lhsT=ident[:], rhs=ident[:], start=True, stop=True)
        for i in range(WARM_BEHIND_Y):
            nc.tensor.matmul(out=warm[:], lhsT=ident[:], rhs=y_sb[:, 0:P], start=True, stop=True)

        def flip_f(n):
            flips = []
            for h in range(HALVES):
                for b in range(2):
                    words = f_raws[n][b][:].bitcast(F32).rearrange(
                        "c (i h p s) -> c i h s p", i=2, h=HALVES, p=P, s=2
                    )
                    flip = flip_banks.tile([P, 4, P], F32, tag="flip")
                    for x in range(4):
                        nc.tensor.transpose(out=flip[:, x, :], in_=words[:, x // 2, h, x % 2, :], identity=ident[:])
                    flips.append(flip)
            return flips

        def gather_f(f_grouped, b, flip):
            grouped_words = f_grouped[:].bitcast(F32).rearrange("p (c b x) -> p b c x", b=2, x=4)
            nc.scalar.copy(out=grouped_words[:, b], in_=flip[:].rearrange("p x c -> p c x"))

        def quantise_f(f_grouped):
            f_codes = f_pass.tile([P, C], U32, align_bytes=64)
            f_scales = f_pass.tile([P, C], U8, align_bytes=64)
            nc.vector.quantize_mx(out=f_codes[:].bitcast(E4M3_X4), scales=f_scales[:], in_=f_grouped[:])
            return f_codes, f_scales

        def regroup_dy(dy, n, a):
            g_raw = g_raws[n][a // PAIR]
            mine = slice((a % PAIR) * HALVES, (a % PAIR + 1) * HALVES)
            split = VECTOR_FIELDS if n + 1 < B else VECTOR_FIELDS_LAST
            nc.scalar.copy(
                out=dy[:, mine, split:NO, :].rearrange("p h (c i) r -> p h c r i", i=4),
                in_=g_raw[:, mine, :, split:NO].rearrange("p h r (c i) -> p h c r i", i=4),
            )
            nc.vector.tensor_copy(
                out=dy[:, mine, NS:split, :].rearrange("p h (c i) r -> p h c r i", i=4),
                in_=g_raw[:, mine, :, NS:split].rearrange("p h r (c i) -> p h c r i", i=4),
            )

        def apply_factor(dy, n, u):
            mine = slice(u * PAIR * HALVES, (u + 1) * PAIR * HALVES)
            nc.vector.tensor_tensor(
                out=dy[:, :, 0:NS, :],
                in0=g_raws[n][u][:, :, :, 0:NS].rearrange("p g r j -> p g j r"),
                in1=factor[:].rearrange("p j r (n a) h -> p n (a h) j r", n=B)[:, n, mine],
                op=ALU.mult,
            )

        def quantise_dy(dy, first, count):
            dy_codes = codes.tile([P, count * NO], U32, align_bytes=64, name="dy_codes", tag="dy_codes")
            dy_scales = codes.tile([P, count * NO], U8, align_bytes=64, name="dy_scales", tag="dy_scales")
            nc.vector.quantize_mx(
                out=dy_codes[:].bitcast(E5M2_X4),
                scales=dy_scales[:],
                in_=dy[:, first : first + count].rearrange("p g j r -> p (g j r)"),
            )
            return dy_codes, dy_scales

        sig = const.tile([P, PACK, P], F32)
        nc.scalar.activation(out=sig[:], in_=y_sb[:].rearrange("q (p r) -> q r p", r=PACK), func=ACT.Sigmoid)
        slope_xy = const.tile([P, PACK, P], F32)
        nc.vector.scalar_tensor_tensor(
            out=slope_xy[:], in0=sig[:], scalar=1.0, in1=sig[:], op0=ALU.subtract, op1=ALU.mult
        )
        slope_wh = const.tile([P, PACK, P], F32)
        nc.vector.scalar_tensor_tensor(
            out=slope_wh[:], in0=slope_xy[:], scalar=-8.0, in1=sig[:], op0=ALU.mult, op1=ALU.mult
        )

        flips = flip_f(0)
        f_groupeds = []
        for h in range(HALVES):
            f_grouped = f_pass.tile([P, C * PACK], BF16, align_bytes=64, tag="f_grouped")
            for b in range(2):
                gather_f(f_grouped, b, flips[2 * h + b])
            f_groupeds.append(f_grouped)
        f_mx = [quantise_f(f_groupeds[0])]

        xy_t = flip_banks.tile([P, PACK, B * NA, NS, HALVES], F32, tag="flip")
        wh_t = flip_banks.tile([P, PACK, B * NA, NS, HALVES], F32, tag="flip")
        for r in range(PACK):
            nc.tensor.transpose(
                out=xy_t[:, r].rearrange("p q j h -> p (q j h)"), in_=slope_xy[:, r, :], identity=ident[:]
            )
        for r in range(PACK):
            nc.tensor.transpose(
                out=wh_t[:, r].rearrange("p q j h -> p (q j h)"), in_=slope_wh[:, r, :], identity=ident[:]
            )
        factor = const.tile([P, NS, PACK, B * NA, HALVES], F32)
        for j in range(2):
            nc.vector.tensor_scalar(
                out=factor[:, j], in0=xy_t[:, :, :, j, :], scalar1=-2.0, scalar2=None, op0=ALU.mult
            )
        for w in range(2):
            nc.vector.tensor_tensor(
                out=factor[:, 2 + w].rearrange("p r (n a) h -> p (r n) a h", a=NA),
                in0=wh_t[:, :, :, 2 + w, :].rearrange("p r (n a) h -> p (r n) a h", a=NA),
                in1=anc[:]
                .rearrange("p (a w) -> p w a", w=2)[:, w, :]
                .unsqueeze(1)
                .unsqueeze(3)
                .to_broadcast([P, PACK * B, NA, HALVES]),
                op=ALU.mult,
            )

        f_mx.append(quantise_f(f_groupeds[1]))

        acc = [acc_banks.tile([P, C], F32, name="acc%d" % a, tag="acc%d" % a) for a in range(NA)]

        def finish(n, a, dy):
            dy_codes, dy_scales = quantise_dy(dy, (a % PAIR) * HALVES, HALVES)
            for h in range(HALVES):
                f_codes, f_scales = f_mx[HALVES * n + h]
                fields = slice(h * NO, (h + 1) * NO)
                nc.tensor.matmul_mx(
                    out=acc[a][:],
                    lhsT=dy_codes[:, fields].bitcast(E5M2_X4),
                    lhsT_scale=dy_scales[:, fields],
                    rhs=f_codes[:].bitcast(E4M3_X4),
                    rhs_scale=f_scales[:],
                    start=(n == 0 and h == 0),
                    stop=(n == B - 1 and h == HALVES - 1),
                )

        flips = flip_f(1)
        for n in range(B):
            more_f = n + 1 < B
            dys = []
            f_groupeds = []
            for a in range(NA):
                if a % PAIR == 0:
                    dys.append(g_piece.tile([P, PAIR * HALVES, NO, PACK], BF16, align_bytes=64, name="dy", tag="dy"))
                regroup_dy(dys[a // PAIR], n, a)
                if more_f and a % 2 == 0:
                    f_groupeds.append(f_pass.tile([P, C * PACK], BF16, align_bytes=64, name="f_grouped", tag="f_grouped"))
                if more_f:
                    gather_f(f_groupeds[a // 2], a % 2, flips[a])
                if a == 0:
                    apply_factor(dys[0], n, 0)
                if a > 0:
                    finish(n, a - 1, dys[(a - 1) // PAIR])
                if a == 2:
                    apply_factor(dys[1], n, 1)
            if n + 2 < B:
                flips = flip_f(n + 2)
            if more_f:
                f_mx.append(quantise_f(f_groupeds[0]))
            finish(n, NA - 1, dys[1])
            if more_f:
                f_mx.append(quantise_f(f_groupeds[1]))

        for a in range(NA - 1):
            rows = result.tile([P, C], F32)
            nc.scalar.copy(out=rows[:], in_=acc[a][:])
            nc.sync.dma_start(out=out[a * NO : (a + 1) * NO, :], in_=rows[:])
        a = NA - 1
        for part in range(2):
            cols = slice(part * (C // 2), (part + 1) * (C // 2))
            rows_half = result.tile([P, C // 2], F32)
            nc.scalar.copy(out=rows_half[:], in_=acc[a][:, cols])
            nc.sync.dma_start(out=out[a * NO : (a + 1) * NO, cols], in_=rows_half[:])
